import numpy as np
import ml_dtypes


def mxq(x, axis, fmt="e4m3"):
    dtype, down = {"e4m3": (ml_dtypes.float8_e4m3fn, 7), "e5m2": (ml_dtypes.float8_e5m2, 14)}[fmt]
    v = np.moveaxis(np.asarray(x, np.float32).astype(ml_dtypes.bfloat16).astype(np.float64), axis, -1)
    blocks = v.reshape(v.shape[:-1] + (-1, 32))
    amax = np.abs(blocks).max(-1, keepdims=True)
    byte = np.maximum(np.where(amax > 0, np.frexp(amax)[1] - 1 + 127, 0) - down, 1)
    scale = np.exp2(byte - 127.0)
    codes = (blocks / scale).astype(np.float32).astype(dtype).astype(np.float64)
    return np.moveaxis((codes * scale).reshape(v.shape), -1, axis)


WIDE = False


def mx_kscale(k):
    if not WIDE:
        return np.ones(k)
    levels = np.array([10, -10, 5, -5, 0])
    if k % 512:
        return np.exp2(np.random.permutation(np.resize(levels, k // 32))).repeat(32)
    a = np.empty((k // 512, 16))
    for p in range(k // 512):
        a[p, :8] = np.random.permutation(np.resize(levels, 8))
        for g in range(8):
            far = levels[np.abs(levels - a[p, g]) >= 10]
            a[p, g + 8] = far[np.random.randint(len(far))]
    return np.exp2(a.ravel()).repeat(32)


BF16 = ml_dtypes.bfloat16


def bf(x):
    return np.asarray(x, np.float32).astype(BF16)


def f64(x):
    return np.asarray(x).astype(np.float64)


B, HW, C, HID, WS, SS, HEADS = 1, 32, 1024, 2048, 8, 4, 16
L = HW * HW
NH = HW // WS
EPS = 1e-5


def adain(x, scale, shift):
    m = x.mean(2, keepdims=True)
    s = np.std(x, axis=2, keepdims=True, ddof=1) + EPS
    return (x - m) / s * scale + shift


def setup_inputs():
    s = mx_kscale(C)
    return {"o_attn": bf(0.4 * np.random.standard_normal((NH * NH * B, WS * WS, C)) * s),
            "out_w": bf(np.random.standard_normal((C, C)) / np.sqrt(C) / s[None, :]),
            "out_b": bf(0.1 * np.random.standard_normal(C)),
            "ada1_scale": bf(1.0 + 0.1 * np.random.standard_normal((1, L, 1))),
            "ada1_shift": bf(0.1 * np.random.standard_normal((1, L, 1))),
            "x": bf(np.random.standard_normal((B, L, C)))}


def reference(o_attn, out_w, out_b, ada1_scale, ada1_shift, x):
    a = (mxq(f64(o_attn), 2, "e4m3") @ mxq(f64(out_w), 1, "e4m3").T) + f64(out_b)
    a = np.swapaxes(a.reshape(B, NH, NH, WS, WS, C), 2, 3).reshape(B, HW, HW, C)
    a = np.roll(a, (SS, SS), axis=(1, 2)).reshape(B, L, C)
    return f64(x) + adain(a, f64(ada1_scale), f64(ada1_shift))

@@ -1,0 +1,356 @@
+from contextlib import ExitStack
+
+import concourse.mybir as mybir
+from concourse.masks import make_identity
+
+F32 = mybir.dt.float32
+BF16 = mybir.dt.bfloat16
+U32 = mybir.dt.uint32
+U8 = mybir.dt.uint8
+FP8X4 = mybir.dt.float8_e4m3fn_x4
+ALU = mybir.AluOpType
+ACT = mybir.ActivationFunctionType
+
+P = 128
+TOKENS = 1024
+CHANNELS = 1024
+K = 1024
+K_PASS = 4 * P
+PASSES = K // K_PASS
+N_TILE = 512
+N_TILES = CHANNELS // N_TILE
+TOKEN_TILES = TOKENS // P
+GRID = 32
+WINDOW = 8
+SHIFT = 4
+PAIR = 2
+GROUPS = TOKEN_TILES // PAIR
+EPS = 1e-5
+
+FLOPS = 2 * TOKENS * CHANNELS * K
+
+
+def transpose_block(nc, psum, words, order):
+    turned = psum.tile([P, PASSES, 2, P], F32, name="turned")
+    for g in range(PASSES):
+        for u in range(2):
+            every_second = slice(2 * P * g + u, 2 * P * (g + 1), 2)
+            nc.tensor.transpose(turned[:, g, u, :], words[:, every_second], order)
+    return turned
+
+
+def quantise(nc, grouped, codes, scales, columns):
+    for g in range(PASSES):
+        nc.vector.quantize_mx(
+            out=codes[:, g, columns].bitcast(FP8X4),
+            scales=scales[:, g, columns],
+            in_=grouped[:, g, columns, :].rearrange("p c t -> p (c t)"),
+        )
+
+
+def tile_swintransformerblock_pb_kernel(
+    tc, o_attn, out_w, out_b, ada1_scale, ada1_shift, x, out
+):
+    nc = tc.nc
+    attn_rows = o_attn.flatten_outer_dims()
+    x_rows = x.flatten_outer_dims()
+    out_rows = out.flatten_outer_dims()
+
+    with ExitStack() as stack:
+        const = stack.enter_context(tc.tile_pool(name="const", bufs=1))
+        keep = stack.enter_context(tc.tile_pool(name="keep", bufs=1))
+        work = stack.enter_context(tc.tile_pool(name="work", bufs=TOKEN_TILES))
+        psum_turned = stack.enter_context(tc.psum_pool(name="psum_turned", bufs=4))
+        psum_acc = stack.enter_context(tc.psum_pool(name="psum_acc", bufs=4))
+        stack.enter_context(tc.manual_schedule())
+
+        bias_row = const.tile([P, CHANNELS], BF16)
+        nc.vector.memset(bias_row[:], 0.0)
+        ada_rows = const.tile([P, P], BF16)
+        nc.vector.memset(ada_rows[:], 0.0)
+        nc.scalar.dma_start(out=bias_row[0:1, :], in_=out_b.unsqueeze(0))
+        for first, vector in ((0, ada1_scale), (TOKEN_TILES, ada1_shift)):
+            rows = vector.rearrange("o (t p) i -> (o t) (p i)", p=P)
+            nc.scalar.dma_start(
+                out=ada_rows[first : first + TOKEN_TILES - 1, :], in_=rows[1:TOKEN_TILES, :]
+            )
+            nc.scalar.dma_start(
+                out=ada_rows[first + TOKEN_TILES - 1 : first + TOKEN_TILES, :], in_=rows[0:1, :]
+            )
+
+        warm = const.tile([P, 1], F32)
+        nc.vector.memset(warm[:], 1.0)
+        nc.scalar.activation(out=warm[:], in_=warm[:], func=ACT.Sqrt)
+        ones = const.tile([P, P], BF16)
+        nc.vector.memset(ones[:], 1.0)
+
+        identity = const.tile([P, P], F32)
+        make_identity(nc, identity[:])
+        identity_bf16 = const.tile([P, P], BF16)
+        nc.vector.tensor_copy(out=identity_bf16[:], in_=identity[:])
+
+        order_left = const.tile([P, P], F32)
+        nc.vector.tensor_copy(
+            out=order_left[:].rearrange("p (r d c) -> p r d c", r=WINDOW, d=2),
+            in_=identity[:].rearrange("p (d r c) -> p r d c", d=2, r=WINDOW),
+        )
+        stay = 2 * WINDOW - SHIFT
+        order_right = const.tile([P, P], F32)
+        staying = order_right[:, 0 : WINDOW * stay].rearrange("p (r j) -> p r j", j=stay)
+        wrapping = order_right[:, WINDOW * stay : P].rearrange("p (r j) -> p r j", j=SHIFT)
+        window2 = identity[:, 0:64].rearrange("p (r c) -> p r c", c=WINDOW)
+        window3 = identity[:, 64:128].rearrange("p (r c) -> p r c", c=WINDOW)
+        nc.vector.tensor_copy(out=staying[:, :, 0:WINDOW], in_=window2)
+        nc.vector.tensor_copy(out=staying[:, :, WINDOW:stay], in_=window3[:, :, 0 : WINDOW - SHIFT])
+        nc.vector.tensor_copy(out=wrapping, in_=window3[:, :, WINDOW - SHIFT : WINDOW])
+
+        w_raw = keep.tile([P, TOKEN_TILES, K], BF16)
+        a_raw = keep.tile([P, TOKEN_TILES, K], BF16)
+        x_sb = keep.tile([P, TOKEN_TILES, CHANNELS], BF16)
+
+        def load_pair(raw, rows, pair):
+            blocks = slice(PAIR * pair, PAIR * pair + PAIR)
+            nc.sync.dma_start(
+                out=raw[:, blocks, :],
+                in_=rows[PAIR * P * pair : PAIR * P * (pair + 1), :].rearrange(
+                    "(b p) k -> p b k", p=P
+                ),
+            )
+
+        def output_rows(tau):
+            first = ((tau + 1) % TOKEN_TILES) * P
+            return slice(first, first + P)
+
+        def load_x(group):
+            for tau in range(PAIR * group, PAIR * group + PAIR):
+                nc.sync.dma_start(out=x_sb[:, tau, :], in_=x_rows[output_rows(tau), :])
+
+        load_pair(a_raw, attn_rows, 0)
+        for pair in range(GROUPS):
+            load_pair(w_raw, out_w, pair)
+        for group in range(1, GROUPS):
+            load_pair(a_raw, attn_rows, group)
+        for group in range(GROUPS):
+            load_x(group)
+
+        w_grouped = keep.tile([P, PASSES, CHANNELS, 4], BF16, align_bytes=64)
+        w_codes = keep.tile([P, PASSES, CHANNELS], U32, align_bytes=64)
+        w_scales = keep.tile([P, PASSES, CHANNELS], U8, align_bytes=64)
+        a_grouped = keep.tile([P, PASSES, TOKENS, 4], BF16, align_bytes=64)
+        a_codes = keep.tile([P, PASSES, TOKENS], U32, align_bytes=64)
+        a_scales = keep.tile([P, PASSES, TOKENS], U8, align_bytes=64)
+        w_words = w_grouped[:].bitcast(F32)
+        a_grid = a_grouped[:].bitcast(F32).rearrange("p g (i j) u -> p g i j u", j=GRID)
+
+        def turn_weights(pair):
+            for block in range(PAIR * pair, PAIR * pair + PAIR):
+                turned = transpose_block(
+                    nc, psum_turned, w_raw[:, block, :].bitcast(F32), identity[:]
+                )
+                nc.scalar.copy(
+                    out=w_words[:, :, block * P : (block + 1) * P, :],
+                    in_=turned[:].rearrange("p g u c -> p g c u"),
+                )
+
+        def quantise_weights(pair):
+            quantise(nc, w_grouped, w_codes, w_scales, slice(PAIR * P * pair, PAIR * P * (pair + 1)))
+
+        def turn_tokens(group):
+            grid_rows = slice(WINDOW * group, WINDOW * (group + 1))
+            left = transpose_block(
+                nc, psum_turned, a_raw[:, PAIR * group, :].bitcast(F32), order_left[:]
+            )
+            nc.scalar.copy(
+                out=a_grid[:, :, grid_rows, SHIFT : SHIFT + 2 * WINDOW, :],
+                in_=left[:].rearrange("p g u (r j) -> p g r j u", j=2 * WINDOW),
+            )
+            right = transpose_block(
+                nc, psum_turned, a_raw[:, PAIR * group + 1, :].bitcast(F32), order_right[:]
+            )
+            nc.scalar.copy(
+                out=a_grid[:, :, grid_rows, GRID - stay : GRID, :],
+                in_=right[:, :, :, 0 : WINDOW * stay].rearrange("p g u (r j) -> p g r j u", j=stay),
+            )
+            nc.scalar.copy(
+                out=a_grid[:, :, grid_rows, 0:SHIFT, :],
+                in_=right[:, :, :, WINDOW * stay : P].rearrange("p g u (r j) -> p g r j u", j=SHIFT),
+            )
+
+        def quantise_tokens(group):
+            quantise(nc, a_grouped, a_codes, a_scales, slice(PAIR * P * group, PAIR * P * (group + 1)))
+
+        bias_all = const.tile([P, CHANNELS], F32)
+        ada = const.tile([P, 2 * TOKEN_TILES], F32)
+        ada_gain = ada[:, 0:TOKEN_TILES]
+        ada_offset = ada[:, TOKEN_TILES : 2 * TOKEN_TILES]
+        inv_ada_gain = const.tile([P, TOKEN_TILES], F32)
+
+        def spread_small_vectors():
+            for n in range(N_TILES):
+                columns = slice(n * N_TILE, (n + 1) * N_TILE)
+                spread = psum_acc.tile([P, N_TILE], F32, name="acc")
+                nc.tensor.matmul(
+                    out=spread[:], lhsT=ones[:], rhs=bias_row[:, columns], start=True, stop=True
+                )
+                nc.vector.tensor_copy(out=bias_all[:, columns], in_=spread[:])
+            ada_turned = psum_turned.tile([P, P], BF16, name="turned")
+            nc.tensor.transpose(ada_turned[:], ada_rows[:], identity_bf16[:])
+            nc.vector.tensor_copy(out=ada[:], in_=ada_turned[:, 0 : 2 * TOKEN_TILES])
+            nc.vector.reciprocal(out=inv_ada_gain[:], in_=ada_gain)
+
+        sums = const.tile([P, TOKEN_TILES, N_TILES], F32)
+        scaled_sums = const.tile([P, TOKEN_TILES, N_TILES], F32)
+        minus_mean = const.tile([P, TOKEN_TILES], F32)
+        squares = const.tile([P, TOKEN_TILES], F32)
+        std = const.tile([P, TOKEN_TILES], F32)
+        gain = const.tile([P, TOKEN_TILES], F32)
+        offset = const.tile([P, TOKEN_TILES], F32)
+        projected = {}
+        result = {}
+
+        acc = {}
+
+        def matmuls(group, n):
+            columns = slice(n * N_TILE, (n + 1) * N_TILE)
+            for tau in range(PAIR * group, PAIR * group + PAIR):
+                tokens = slice(tau * P, (tau + 1) * P)
+                acc[tau, n] = psum_acc.tile([P, N_TILE], F32, name="acc")
+                for g in range(PASSES):
+                    nc.tensor.matmul_mx(
+                        out=acc[tau, n][:],
+                        lhsT=a_codes[:, g, tokens].bitcast(FP8X4),
+                        lhsT_scale=a_scales[:, g, tokens],
+                        rhs=w_codes[:, g, columns].bitcast(FP8X4),
+                        rhs_scale=w_scales[:, g, columns],
+                        start=(g == 0),
+                        stop=(g == PASSES - 1),
+                    )
+
+        def add_bias(group, n):
+            columns = slice(n * N_TILE, (n + 1) * N_TILE)
+            for tau in range(PAIR * group, PAIR * group + PAIR):
+                if n == 0:
+                    projected[tau] = work.tile([P, CHANNELS], F32, name="projected")
+                nc.vector.scalar_tensor_tensor(
+                    out=projected[tau][:, columns],
+                    in0=acc[tau, n][:],
+                    scalar=1.0,
+                    in1=bias_all[:, columns],
+                    op0=ALU.mult,
+                    op1=ALU.add,
+                    accum_out=sums[:, tau, n : n + 1],
+                )
+
+        def statistics(group):
+            pair = slice(PAIR * group, PAIR * group + PAIR)
+            for tau in range(PAIR * group, PAIR * group + PAIR):
+                nc.scalar.activation(
+                    out=scaled_sums[:, tau, :],
+                    in_=sums[:, tau, :],
+                    func=ACT.Identity,
+                    scale=-1.0 / CHANNELS,
+                    accum_out=minus_mean[:, tau : tau + 1],
+                )
+                deviation_squared = work.tile([P, CHANNELS], BF16, name="deviation_squared")
+                nc.scalar.activation(
+                    out=deviation_squared[:],
+                    in_=projected[tau][:],
+                    func=ACT.Square,
+                    bias=minus_mean[:, tau : tau + 1],
+                    accum_out=squares[:, tau : tau + 1],
+                )
+            nc.scalar.activation(
+                out=std[:, pair], in_=squares[:, pair], func=ACT.Sqrt, scale=1.0 / (CHANNELS - 1)
+            )
+
+        def shift_residual(group):
+            pair = slice(PAIR * group, PAIR * group + PAIR)
+            nc.vector.scalar_tensor_tensor(
+                out=gain[:, pair],
+                in0=std[:, pair],
+                scalar=EPS,
+                in1=inv_ada_gain[:, pair],
+                op0=ALU.add,
+                op1=ALU.mult,
+            )
+            nc.vector.reciprocal(out=gain[:, pair], in_=gain[:, pair])
+            for tau in range(PAIR * group, PAIR * group + PAIR):
+                nc.vector.tensor_scalar(
+                    out=offset[:, tau : tau + 1],
+                    in0=minus_mean[:, tau : tau + 1],
+                    scalar1=gain[:, tau : tau + 1],
+                    scalar2=ada_offset[:, tau : tau + 1],
+                    op0=ALU.mult,
+                    op1=ALU.add,
+                )
+            for tau in range(PAIR * group, PAIR * group + PAIR):
+                result[tau] = work.tile([P, CHANNELS], F32, name="result")
+                if tau < TOKEN_TILES // 2:
+                    nc.gpsimd.tensor_scalar(
+                        out=result[tau][:],
+                        in0=x_sb[:, tau, :],
+                        scalar1=1.0,
+                        scalar2=offset[:, tau : tau + 1],
+                        op0=ALU.mult,
+                        op1=ALU.add,
+                    )
+                else:
+                    nc.scalar.activation(
+                        out=result[tau][:],
+                        in_=x_sb[:, tau, :],
+                        func=ACT.Identity,
+                        bias=offset[:, tau : tau + 1],
+                    )
+
+        def finish(group):
+            for tau in range(PAIR * group, PAIR * group + PAIR):
+                pieces = 2 if tau == TOKEN_TILES - 1 else 1
+                width = CHANNELS // pieces
+                for piece in range(pieces):
+                    columns = slice(piece * width, (piece + 1) * width)
+                    nc.vector.scalar_tensor_tensor(
+                        out=result[tau][:, columns],
+                        in0=projected[tau][:, columns],
+                        scalar=gain[:, tau : tau + 1],
+                        in1=result[tau][:, columns],
+                        op0=ALU.mult,
+                        op1=ALU.add,
+                    )
+                    nc.sync.dma_start(
+                        out=out_rows[output_rows(tau), columns], in_=result[tau][:, columns]
+                    )
+
+        turn_tokens(0)
+        quantise_tokens(0)
+        turn_weights(0)
+        spread_small_vectors()
+        quantise_weights(0)
+        turn_weights(1)
+        quantise_weights(1)
+        turn_weights(2)
+        matmuls(0, 0)
+        quantise_weights(2)
+        turn_weights(3)
+        add_bias(0, 0)
+        quantise_weights(3)
+        turn_tokens(1)
+        turn_tokens(2)
+        quantise_tokens(1)
+        matmuls(0, 1)
+        turn_tokens(3)
+        add_bias(0, 1)
+        statistics(0)
+        quantise_tokens(2)
+        for step in range(1, GROUPS + 3):
+            if step < GROUPS:
+                for n in range(N_TILES):
+                    matmuls(step, n)
+                for n in range(N_TILES):
+                    add_bias(step, n)
+                statistics(step)
+            if step + 2 < GROUPS:
+                quantise_tokens(step + 2)
+            if step >= 3:
+                finish(step - 3)
+            if step <= GROUPS:
+                shift_residual(step - 1)

@@ -30,22 +30,11 @@ EPS = 1e-5
 FLOPS = 2 * TOKENS * CHANNELS * K
 
 
-def transpose_block(nc, psum, words, order):
-    turned = psum.tile([P, PASSES, 2, P], F32, name="turned")
+def transpose_block(nc, words, order, places):
     for g in range(PASSES):
         for u in range(2):
             every_second = slice(2 * P * g + u, 2 * P * (g + 1), 2)
-            nc.tensor.transpose(turned[:, g, u, :], words[:, every_second], order)
-    return turned
-
-
-def quantise(nc, grouped, codes, scales, columns):
-    for g in range(PASSES):
-        nc.vector.quantize_mx(
-            out=codes[:, g, columns].bitcast(FP8X4),
-            scales=scales[:, g, columns],
-            in_=grouped[:, g, columns, :].rearrange("p c t -> p (c t)"),
-        )
+            nc.tensor.transpose(places[g][u], words[:, every_second], order)
 
 
 def tile_swintransformerblock_pb_kernel(
@@ -59,28 +48,26 @@ def tile_swintransformerblock_pb_kernel(
     with ExitStack() as stack:
         const = stack.enter_context(tc.tile_pool(name="const", bufs=1))
         keep = stack.enter_context(tc.tile_pool(name="keep", bufs=1))
-        work = stack.enter_context(tc.tile_pool(name="work", bufs=TOKEN_TILES))
+        work = stack.enter_context(tc.tile_pool(name="work", bufs=2 * GROUPS * PASSES))
         psum_turned = stack.enter_context(tc.psum_pool(name="psum_turned", bufs=4))
         psum_acc = stack.enter_context(tc.psum_pool(name="psum_acc", bufs=4))
         stack.enter_context(tc.manual_schedule())
 
-        bias_row = const.tile([P, CHANNELS], BF16)
-        nc.vector.memset(bias_row[:], 0.0)
-        ada_rows = const.tile([P, P], BF16)
-        nc.vector.memset(ada_rows[:], 0.0)
-        nc.scalar.dma_start(out=bias_row[0:1, :], in_=out_b.unsqueeze(0))
-        for first, vector in ((0, ada1_scale), (TOKEN_TILES, ada1_shift)):
-            rows = vector.rearrange("o (t p) i -> (o t) (p i)", p=P)
-            nc.scalar.dma_start(
-                out=ada_rows[first : first + TOKEN_TILES - 1, :], in_=rows[1:TOKEN_TILES, :]
-            )
-            nc.scalar.dma_start(
-                out=ada_rows[first + TOKEN_TILES - 1 : first + TOKEN_TILES, :], in_=rows[0:1, :]
-            )
-
         warm = const.tile([P, 1], F32)
         nc.vector.memset(warm[:], 1.0)
         nc.scalar.activation(out=warm[:], in_=warm[:], func=ACT.Sqrt)
+
+        ada_rows = const.tile([P, P], BF16)
+        nc.vector.memset(ada_rows[:].bitcast(U32), 0)
+        bias_row = const.tile([P, CHANNELS], BF16)
+        nc.vector.memset(bias_row[:].bitcast(U32), 0)
+        for first, vector in ((0, ada1_scale), (TOKEN_TILES, ada1_shift)):
+            nc.scalar.dma_start(
+                out=ada_rows[first : first + TOKEN_TILES, :],
+                in_=vector.rearrange("o (t p) i -> (o t) (p i)", p=P),
+            )
+        nc.scalar.dma_start(out=bias_row[0:1, :], in_=out_b.unsqueeze(0))
+
         ones = const.tile([P, P], BF16)
         nc.vector.memset(ones[:], 1.0)
 
@@ -94,19 +81,25 @@ def tile_swintransformerblock_pb_kernel(
             out=order_left[:].rearrange("p (r d c) -> p r d c", r=WINDOW, d=2),
             in_=identity[:].rearrange("p (d r c) -> p r d c", d=2, r=WINDOW),
         )
-        stay = 2 * WINDOW - SHIFT
+        stay = WINDOW - SHIFT
         order_right = const.tile([P, P], F32)
-        staying = order_right[:, 0 : WINDOW * stay].rearrange("p (r j) -> p r j", j=stay)
-        wrapping = order_right[:, WINDOW * stay : P].rearrange("p (r j) -> p r j", j=SHIFT)
+        runs = order_right[:].rearrange("p (r j) -> p r j", j=2 * WINDOW)
         window2 = identity[:, 0:64].rearrange("p (r c) -> p r c", c=WINDOW)
         window3 = identity[:, 64:128].rearrange("p (r c) -> p r c", c=WINDOW)
-        nc.vector.tensor_copy(out=staying[:, :, 0:WINDOW], in_=window2)
-        nc.vector.tensor_copy(out=staying[:, :, WINDOW:stay], in_=window3[:, :, 0 : WINDOW - SHIFT])
-        nc.vector.tensor_copy(out=wrapping, in_=window3[:, :, WINDOW - SHIFT : WINDOW])
+        nc.vector.tensor_copy(out=runs[:, :, 0:WINDOW], in_=window2)
+        nc.vector.tensor_copy(out=runs[:, :, WINDOW : WINDOW + stay], in_=window3[:, :, 0:stay])
+        for above, row, rows in ((0, 1, WINDOW - 1), (WINDOW - 1, 0, 1)):
+            nc.vector.tensor_copy(
+                out=runs[:, above : above + rows, WINDOW + stay :],
+                in_=window3[:, row : row + rows, stay:],
+            )
 
         w_raw = keep.tile([P, TOKEN_TILES, K], BF16)
         a_raw = keep.tile([P, TOKEN_TILES, K], BF16)
         x_sb = keep.tile([P, TOKEN_TILES, CHANNELS], BF16)
+
+        def load_block(raw, rows, block):
+            nc.sync.dma_start(out=raw[:, block, :], in_=rows[P * block : P * (block + 1), :])
 
         def load_pair(raw, rows, pair):
             blocks = slice(PAIR * pair, PAIR * pair + PAIR)
@@ -125,64 +118,83 @@ def tile_swintransformerblock_pb_kernel(
             for tau in range(PAIR * group, PAIR * group + PAIR):
                 nc.sync.dma_start(out=x_sb[:, tau, :], in_=x_rows[output_rows(tau), :])
 
-        load_pair(a_raw, attn_rows, 0)
-        for pair in range(GROUPS):
-            load_pair(w_raw, out_w, pair)
-        for group in range(1, GROUPS):
-            load_pair(a_raw, attn_rows, group)
+        load_block(a_raw, attn_rows, 0)
+        load_block(a_raw, attn_rows, 1)
+        load_pair(w_raw, out_w, 0)
+        load_pair(w_raw, out_w, 1)
+        load_pair(a_raw, attn_rows, 1)
+        load_pair(w_raw, out_w, 2)
+        load_pair(w_raw, out_w, 3)
+        load_pair(a_raw, attn_rows, 2)
+        load_pair(a_raw, attn_rows, 3)
         for group in range(GROUPS):
             load_x(group)
 
-        w_grouped = keep.tile([P, PASSES, CHANNELS, 4], BF16, align_bytes=64)
         w_codes = keep.tile([P, PASSES, CHANNELS], U32, align_bytes=64)
         w_scales = keep.tile([P, PASSES, CHANNELS], U8, align_bytes=64)
-        a_grouped = keep.tile([P, PASSES, TOKENS, 4], BF16, align_bytes=64)
         a_codes = keep.tile([P, PASSES, TOKENS], U32, align_bytes=64)
         a_scales = keep.tile([P, PASSES, TOKENS], U8, align_bytes=64)
-        w_words = w_grouped[:].bitcast(F32)
-        a_grid = a_grouped[:].bitcast(F32).rearrange("p g (i j) u -> p g i j u", j=GRID)
+        grouped = {}
 
-        def turn_weights(pair):
-            for block in range(PAIR * pair, PAIR * pair + PAIR):
-                turned = transpose_block(
-                    nc, psum_turned, w_raw[:, block, :].bitcast(F32), identity[:]
+        def turned_pair(operand, pair):
+            banks = []
+            for g in range(PASSES):
+                banks.append(psum_turned.tile([P, 2, PAIR * P], F32, name="turned"))
+                grouped[operand, pair, g] = work.tile(
+                    [P, PAIR * P, 4], BF16, name="grouped", align_bytes=64
                 )
-                nc.scalar.copy(
-                    out=w_words[:, :, block * P : (block + 1) * P, :],
-                    in_=turned[:].rearrange("p g u c -> p g c u"),
+            return banks
+
+        def words_of(operand, pair, g):
+            return grouped[operand, pair, g][:].rearrange("p c t -> p (c t)").bitcast(F32).rearrange(
+                "p (c u) -> p c u", u=2
+            )
+
+        def turn_weights(pair, copies):
+            banks = turned_pair("w", pair)
+            for half in range(PAIR):
+                columns = slice(half * P, (half + 1) * P)
+                transpose_block(
+                    nc,
+                    w_raw[:, PAIR * pair + half, :].bitcast(F32),
+                    identity[:],
+                    [[bank[:, u, columns] for u in range(2)] for bank in banks],
+                )
+            for g in range(PASSES):
+                copies[g](
+                    out=words_of("w", pair, g), in_=banks[g][:].rearrange("p u c -> p c u")
                 )
 
-        def quantise_weights(pair):
-            quantise(nc, w_grouped, w_codes, w_scales, slice(PAIR * P * pair, PAIR * P * (pair + 1)))
+        def turn_tokens(group, copies):
+            banks = turned_pair("a", group)
+            rows = [bank[:].rearrange("p u (r j) -> p u r j", j=GRID) for bank in banks]
+            for half, order in ((0, order_left), (1, order_right)):
+                columns = slice(half * 2 * WINDOW, (half + 1) * 2 * WINDOW)
+                transpose_block(
+                    nc,
+                    a_raw[:, PAIR * group + half, :].bitcast(F32),
+                    order[:],
+                    [[row[:, u, :, columns] for u in range(2)] for row in rows],
+                )
+            for g in range(PASSES):
+                words = words_of("a", group, g)
+                turned = banks[g][:].rearrange("p u c -> p c u")
+                copies[g](out=words[:, SHIFT:, :], in_=turned[:, : PAIR * P - SHIFT, :])
+                copies[g](out=words[:, :SHIFT, :], in_=turned[:, PAIR * P - SHIFT :, :])
 
-        def turn_tokens(group):
-            grid_rows = slice(WINDOW * group, WINDOW * (group + 1))
-            left = transpose_block(
-                nc, psum_turned, a_raw[:, PAIR * group, :].bitcast(F32), order_left[:]
+        def quantise(operand, pair, g):
+            codes, scales = (w_codes, w_scales) if operand == "w" else (a_codes, a_scales)
+            columns = slice(PAIR * P * pair, PAIR * P * (pair + 1))
+            nc.vector.quantize_mx(
+                out=codes[:, g, columns].bitcast(FP8X4),
+                scales=scales[:, g, columns],
+                in_=grouped[operand, pair, g][:].rearrange("p c t -> p (c t)"),
             )
-            nc.scalar.copy(
-                out=a_grid[:, :, grid_rows, SHIFT : SHIFT + 2 * WINDOW, :],
-                in_=left[:].rearrange("p g u (r j) -> p g r j u", j=2 * WINDOW),
-            )
-            right = transpose_block(
-                nc, psum_turned, a_raw[:, PAIR * group + 1, :].bitcast(F32), order_right[:]
-            )
-            nc.scalar.copy(
-                out=a_grid[:, :, grid_rows, GRID - stay : GRID, :],
-                in_=right[:, :, :, 0 : WINDOW * stay].rearrange("p g u (r j) -> p g r j u", j=stay),
-            )
-            nc.scalar.copy(
-                out=a_grid[:, :, grid_rows, 0:SHIFT, :],
-                in_=right[:, :, :, WINDOW * stay : P].rearrange("p g u (r j) -> p g r j u", j=SHIFT),
-            )
-
-        def quantise_tokens(group):
-            quantise(nc, a_grouped, a_codes, a_scales, slice(PAIR * P * group, PAIR * P * (group + 1)))
 
         bias_all = const.tile([P, CHANNELS], F32)
-        ada = const.tile([P, 2 * TOKEN_TILES], F32)
-        ada_gain = ada[:, 0:TOKEN_TILES]
-        ada_offset = ada[:, TOKEN_TILES : 2 * TOKEN_TILES]
+        ada = const.tile([P, 2, TOKEN_TILES + 1], F32)
+        ada_gain = ada[:, 0, 1:]
+        ada_offset = ada[:, 1, 1:]
         inv_ada_gain = const.tile([P, TOKEN_TILES], F32)
 
         def spread_small_vectors():
@@ -195,7 +207,9 @@ def tile_swintransformerblock_pb_kernel(
                 nc.vector.tensor_copy(out=bias_all[:, columns], in_=spread[:])
             ada_turned = psum_turned.tile([P, P], BF16, name="turned")
             nc.tensor.transpose(ada_turned[:], ada_rows[:], identity_bf16[:])
-            nc.vector.tensor_copy(out=ada[:], in_=ada_turned[:, 0 : 2 * TOKEN_TILES])
+            vectors = ada_turned[:, 0 : 2 * TOKEN_TILES].rearrange("p (s t) -> p s t", s=2)
+            nc.vector.tensor_copy(out=ada[:, :, 0:TOKEN_TILES], in_=vectors)
+            nc.vector.tensor_copy(out=ada[:, :, TOKEN_TILES:], in_=vectors[:, :, 0:1])
             nc.vector.reciprocal(out=inv_ada_gain[:], in_=ada_gain)
 
         sums = const.tile([P, TOKEN_TILES, N_TILES], F32)
@@ -210,61 +224,63 @@ def tile_swintransformerblock_pb_kernel(
 
         acc = {}
 
-        def matmuls(group, n):
+        def matmuls(tau, n):
             columns = slice(n * N_TILE, (n + 1) * N_TILE)
-            for tau in range(PAIR * group, PAIR * group + PAIR):
-                tokens = slice(tau * P, (tau + 1) * P)
-                acc[tau, n] = psum_acc.tile([P, N_TILE], F32, name="acc")
-                for g in range(PASSES):
-                    nc.tensor.matmul_mx(
-                        out=acc[tau, n][:],
-                        lhsT=a_codes[:, g, tokens].bitcast(FP8X4),
-                        lhsT_scale=a_scales[:, g, tokens],
-                        rhs=w_codes[:, g, columns].bitcast(FP8X4),
-                        rhs_scale=w_scales[:, g, columns],
-                        start=(g == 0),
-                        stop=(g == PASSES - 1),
-                    )
-
-        def add_bias(group, n):
-            columns = slice(n * N_TILE, (n + 1) * N_TILE)
-            for tau in range(PAIR * group, PAIR * group + PAIR):
-                if n == 0:
-                    projected[tau] = work.tile([P, CHANNELS], F32, name="projected")
-                nc.vector.scalar_tensor_tensor(
-                    out=projected[tau][:, columns],
-                    in0=acc[tau, n][:],
-                    scalar=1.0,
-                    in1=bias_all[:, columns],
-                    op0=ALU.mult,
-                    op1=ALU.add,
-                    accum_out=sums[:, tau, n : n + 1],
+            tokens = slice(tau * P, (tau + 1) * P)
+            acc[tau, n] = psum_acc.tile([P, N_TILE], F32, name="acc")
+            for g in range(PASSES):
+                nc.tensor.matmul_mx(
+                    out=acc[tau, n][:],
+                    lhsT=a_codes[:, g, tokens].bitcast(FP8X4),
+                    lhsT_scale=a_scales[:, g, tokens],
+                    rhs=w_codes[:, g, columns].bitcast(FP8X4),
+                    rhs_scale=w_scales[:, g, columns],
+                    start=(g == 0),
+                    stop=(g == PASSES - 1),
                 )
 
-        def statistics(group):
-            pair = slice(PAIR * group, PAIR * group + PAIR)
-            for tau in range(PAIR * group, PAIR * group + PAIR):
-                nc.scalar.activation(
-                    out=scaled_sums[:, tau, :],
-                    in_=sums[:, tau, :],
-                    func=ACT.Identity,
-                    scale=-1.0 / CHANNELS,
-                    accum_out=minus_mean[:, tau : tau + 1],
-                )
-                deviation_squared = work.tile([P, CHANNELS], BF16, name="deviation_squared")
-                nc.scalar.activation(
-                    out=deviation_squared[:],
-                    in_=projected[tau][:],
-                    func=ACT.Square,
-                    bias=minus_mean[:, tau : tau + 1],
-                    accum_out=squares[:, tau : tau + 1],
-                )
+        def add_bias(tau, n):
+            columns = slice(n * N_TILE, (n + 1) * N_TILE)
+            if n == 0:
+                projected[tau] = work.tile([P, CHANNELS], F32, name="projected", bufs=TOKEN_TILES)
+            nc.vector.scalar_tensor_tensor(
+                out=projected[tau][:, columns],
+                in0=acc[tau, n][:],
+                scalar=1.0,
+                in1=bias_all[:, columns],
+                op0=ALU.mult,
+                op1=ALU.add,
+                accum_out=sums[:, tau, n : n + 1],
+            )
+
+        def deviations(tau):
+            nc.scalar.activation(
+                out=scaled_sums[:, tau, :],
+                in_=sums[:, tau, :],
+                func=ACT.Identity,
+                scale=-1.0 / CHANNELS,
+                accum_out=minus_mean[:, tau : tau + 1],
+            )
+            deviation_squared = work.tile([P, CHANNELS], BF16, name="deviation_squared", bufs=2)
+            nc.scalar.activation(
+                out=deviation_squared[:],
+                in_=projected[tau][:],
+                func=ACT.Square,
+                bias=minus_mean[:, tau : tau + 1],
+                accum_out=squares[:, tau : tau + 1],
+            )
+
+        def pair_columns(group):
+            return slice(PAIR * group, PAIR * group + PAIR)
+
+        def deviation(group):
+            pair = pair_columns(group)
             nc.scalar.activation(
                 out=std[:, pair], in_=squares[:, pair], func=ACT.Sqrt, scale=1.0 / (CHANNELS - 1)
             )
 
-        def shift_residual(group):
-            pair = slice(PAIR * group, PAIR * group + PAIR)
+        def inverse_gain(group):
+            pair = pair_columns(group)
             nc.vector.scalar_tensor_tensor(
                 out=gain[:, pair],
                 in0=std[:, pair],
@@ -273,7 +289,12 @@ def tile_swintransformerblock_pb_kernel(
                 op0=ALU.add,
                 op1=ALU.mult,
             )
+
+        def turn_gain(group):
+            pair = pair_columns(group)
             nc.vector.reciprocal(out=gain[:, pair], in_=gain[:, pair])
+
+        def offsets(group):
             for tau in range(PAIR * group, PAIR * group + PAIR):
                 nc.vector.tensor_scalar(
                     out=offset[:, tau : tau + 1],
@@ -283,74 +304,132 @@ def tile_swintransformerblock_pb_kernel(
                     op0=ALU.mult,
                     op1=ALU.add,
                 )
-            for tau in range(PAIR * group, PAIR * group + PAIR):
-                result[tau] = work.tile([P, CHANNELS], F32, name="result")
-                if tau < TOKEN_TILES // 2:
-                    nc.gpsimd.tensor_scalar(
-                        out=result[tau][:],
-                        in0=x_sb[:, tau, :],
-                        scalar1=1.0,
-                        scalar2=offset[:, tau : tau + 1],
-                        op0=ALU.mult,
-                        op1=ALU.add,
-                    )
-                else:
-                    nc.scalar.activation(
-                        out=result[tau][:],
-                        in_=x_sb[:, tau, :],
-                        func=ACT.Identity,
-                        bias=offset[:, tau : tau + 1],
-                    )
 
-        def finish(group):
-            for tau in range(PAIR * group, PAIR * group + PAIR):
-                pieces = 2 if tau == TOKEN_TILES - 1 else 1
-                width = CHANNELS // pieces
-                for piece in range(pieces):
-                    columns = slice(piece * width, (piece + 1) * width)
-                    nc.vector.scalar_tensor_tensor(
-                        out=result[tau][:, columns],
-                        in0=projected[tau][:, columns],
-                        scalar=gain[:, tau : tau + 1],
-                        in1=result[tau][:, columns],
-                        op0=ALU.mult,
-                        op1=ALU.add,
-                    )
-                    nc.sync.dma_start(
-                        out=out_rows[output_rows(tau), columns], in_=result[tau][:, columns]
-                    )
+        def shift_residual(tau):
+            result[tau] = work.tile([P, CHANNELS], F32, name="result", bufs=TOKEN_TILES)
+            if tau < TOKEN_TILES // 2:
+                nc.gpsimd.tensor_scalar(
+                    out=result[tau][:],
+                    in0=x_sb[:, tau, :],
+                    scalar1=1.0,
+                    scalar2=offset[:, tau : tau + 1],
+                    op0=ALU.mult,
+                    op1=ALU.add,
+                )
+            else:
+                nc.scalar.activation(
+                    out=result[tau][:],
+                    in_=x_sb[:, tau, :],
+                    func=ACT.Identity,
+                    bias=offset[:, tau : tau + 1],
+                )
 
-        turn_tokens(0)
-        quantise_tokens(0)
-        turn_weights(0)
+        def finish(tau):
+            pieces = 2 if tau == TOKEN_TILES - 1 else 1
+            width = CHANNELS // pieces
+            for piece in range(pieces):
+                columns = slice(piece * width, (piece + 1) * width)
+                nc.vector.scalar_tensor_tensor(
+                    out=result[tau][:, columns],
+                    in0=projected[tau][:, columns],
+                    scalar=gain[:, tau : tau + 1],
+                    in1=result[tau][:, columns],
+                    op0=ALU.mult,
+                    op1=ALU.add,
+                )
+                nc.sync.dma_start(
+                    out=out_rows[output_rows(tau), columns], in_=result[tau][:, columns]
+                )
+
+        on_scalar = nc.scalar.copy
+        on_vector = nc.vector.tensor_copy
+
+        def quantise_pair(operand, pair):
+            for g in range(PASSES):
+                quantise(operand, pair, g)
+
+        turn_tokens(0, (on_scalar, on_vector))
+        quantise_pair("a", 0)
+        turn_weights(0, (on_scalar, on_vector))
         spread_small_vectors()
-        quantise_weights(0)
-        turn_weights(1)
-        quantise_weights(1)
-        turn_weights(2)
+        quantise_pair("w", 0)
+        turn_weights(1, (on_scalar, on_vector))
+        quantise_pair("w", 1)
+        turn_tokens(1, (on_scalar, on_scalar))
         matmuls(0, 0)
-        quantise_weights(2)
-        turn_weights(3)
+        matmuls(1, 0)
         add_bias(0, 0)
-        quantise_weights(3)
-        turn_tokens(1)
-        turn_tokens(2)
-        quantise_tokens(1)
-        matmuls(0, 1)
-        turn_tokens(3)
+        add_bias(1, 0)
+        quantise_pair("a", 1)
+        turn_weights(2, (on_scalar, on_scalar))
+        matmuls(2, 0)
+        matmuls(3, 0)
+        quantise_pair("w", 2)
+        add_bias(2, 0)
+        add_bias(3, 0)
+        turn_weights(3, (on_scalar, on_scalar))
+        quantise_pair("w", 3)
+        turn_tokens(2, (on_scalar, on_scalar))
+        for tau in range(4):
+            matmuls(tau, 1)
         add_bias(0, 1)
-        statistics(0)
-        quantise_tokens(2)
-        for step in range(1, GROUPS + 3):
-            if step < GROUPS:
-                for n in range(N_TILES):
-                    matmuls(step, n)
-                for n in range(N_TILES):
-                    add_bias(step, n)
-                statistics(step)
-            if step + 2 < GROUPS:
-                quantise_tokens(step + 2)
-            if step >= 3:
-                finish(step - 3)
-            if step <= GROUPS:
-                shift_residual(step - 1)
+        deviations(0)
+        add_bias(1, 1)
+        deviations(1)
+        quantise_pair("a", 2)
+        deviation(0)
+        turn_tokens(3, (on_scalar, on_scalar))
+        add_bias(2, 1)
+        add_bias(3, 1)
+        quantise_pair("a", 3)
+        deviations(2)
+        deviations(3)
+        deviation(1)
+        for tau in (4, 5):
+            for n in range(N_TILES):
+                matmuls(tau, n)
+        inverse_gain(0)
+        add_bias(4, 0)
+        turn_gain(0)
+        add_bias(4, 1)
+        offsets(0)
+        shift_residual(0)
+        shift_residual(1)
+        deviations(4)
+        add_bias(5, 0)
+        inverse_gain(1)
+        add_bias(5, 1)
+        turn_gain(1)
+        deviations(5)
+        deviation(2)
+        for tau in (6, 7):
+            for n in range(N_TILES):
+                matmuls(tau, n)
+        add_bias(6, 0)
+        offsets(1)
+        shift_residual(2)
+        shift_residual(3)
+        add_bias(6, 1)
+        deviations(6)
+        add_bias(7, 0)
+        add_bias(7, 1)
+        deviations(7)
+        deviation(3)
+        finish(0)
+        inverse_gain(2)
+        finish(1)
+        turn_gain(2)
+        finish(2)
+        offsets(2)
+        shift_residual(4)
+        shift_residual(5)
+        inverse_gain(3)
+        finish(3)
+        turn_gain(3)
+        offsets(3)
+        shift_residual(6)
+        shift_residual(7)
+        finish(4)
+        finish(5)
+        finish(6)
+        finish(7)

@@ -57,6 +57,16 @@ def tile_swintransformerblock_pb_kernel(
         nc.vector.memset(warm[:], 1.0)
         nc.scalar.activation(out=warm[:], in_=warm[:], func=ACT.Sqrt)
 
+        filler = const.tile([P, N_TILE], BF16)
+        nc.vector.memset(filler[:].bitcast(U32), 0)
+
+        def keep_clock_up(times):
+            for step in range(times):
+                idle = psum_acc.tile([P, N_TILE], F32, name="acc")
+                nc.tensor.matmul(
+                    out=idle[:], lhsT=filler[:, 0:P], rhs=filler[:], start=True, stop=True
+                )
+
         ada_rows = const.tile([P, P], BF16)
         nc.vector.memset(ada_rows[:].bitcast(U32), 0)
         bias_row = const.tile([P, CHANNELS], BF16)
@@ -348,14 +358,18 @@ def tile_swintransformerblock_pb_kernel(
             for g in range(PASSES):
                 quantise(operand, pair, g)
 
+        keep_clock_up(4)
         turn_tokens(0, (on_scalar, on_vector))
         quantise_pair("a", 0)
+        keep_clock_up(1)
         turn_weights(0, (on_scalar, on_vector))
         spread_small_vectors()
         quantise_pair("w", 0)
         turn_weights(1, (on_scalar, on_vector))
         quantise_pair("w", 1)
+        keep_clock_up(1)
         turn_tokens(1, (on_scalar, on_scalar))
+        keep_clock_up(1)
         matmuls(0, 0)
         matmuls(1, 0)
         add_bias(0, 0)

@@ -48,7 +48,7 @@ def tile_swintransformerblock_pb_kernel(
     with ExitStack() as stack:
         const = stack.enter_context(tc.tile_pool(name="const", bufs=1))
         keep = stack.enter_context(tc.tile_pool(name="keep", bufs=1))
-        work = stack.enter_context(tc.tile_pool(name="work", bufs=2 * GROUPS * PASSES))
+        work = stack.enter_context(tc.tile_pool(name="work", bufs=TOKEN_TILES))
         psum_turned = stack.enter_context(tc.psum_pool(name="psum_turned", bufs=4))
         psum_acc = stack.enter_context(tc.psum_pool(name="psum_acc", bufs=4))
         stack.enter_context(tc.manual_schedule())
@@ -67,42 +67,36 @@ def tile_swintransformerblock_pb_kernel(
                     out=idle[:], lhsT=filler[:, 0:P], rhs=filler[:], start=True, stop=True
                 )
 
-        ada_rows = const.tile([P, P], BF16)
-        nc.vector.memset(ada_rows[:].bitcast(U32), 0)
-        bias_row = const.tile([P, CHANNELS], BF16)
-        nc.vector.memset(bias_row[:].bitcast(U32), 0)
-        for first, vector in ((0, ada1_scale), (TOKEN_TILES, ada1_shift)):
-            nc.scalar.dma_start(
-                out=ada_rows[first : first + TOKEN_TILES, :],
-                in_=vector.rearrange("o (t p) i -> (o t) (p i)", p=P),
+        vector_rows = const.tile([P, P], BF16)
+        nc.vector.memset(vector_rows[:].bitcast(U32), 0)
+        for index, rows in enumerate(
+            (
+                ada1_scale.rearrange("o (t p) i -> (o t) (p i)", p=P),
+                ada1_shift.rearrange("o (t p) i -> (o t) (p i)", p=P),
+                out_b.rearrange("(t p) -> t p", p=P),
             )
-        nc.scalar.dma_start(out=bias_row[0:1, :], in_=out_b.unsqueeze(0))
-
-        ones = const.tile([P, P], BF16)
-        nc.vector.memset(ones[:], 1.0)
+        ):
+            nc.scalar.dma_start(out=vector_rows[8 * index : 8 * (index + 1), :], in_=rows)
 
         identity = const.tile([P, P], F32)
         make_identity(nc, identity[:])
-        identity_bf16 = const.tile([P, P], BF16)
-        nc.vector.tensor_copy(out=identity_bf16[:], in_=identity[:])
 
         order_left = const.tile([P, P], F32)
         nc.vector.tensor_copy(
             out=order_left[:].rearrange("p (r d c) -> p r d c", r=WINDOW, d=2),
             in_=identity[:].rearrange("p (d r c) -> p r d c", d=2, r=WINDOW),
         )
-        stay = WINDOW - SHIFT
+        stay = 2 * WINDOW - SHIFT
         order_right = const.tile([P, P], F32)
-        runs = order_right[:].rearrange("p (r j) -> p r j", j=2 * WINDOW)
+        staying = order_right[:, 0 : WINDOW * stay].rearrange("p (r j) -> p r j", j=stay)
+        wrapping = order_right[:, WINDOW * stay : P].rearrange("p (r j) -> p r j", j=SHIFT)
         window2 = identity[:, 0:64].rearrange("p (r c) -> p r c", c=WINDOW)
         window3 = identity[:, 64:128].rearrange("p (r c) -> p r c", c=WINDOW)
-        nc.vector.tensor_copy(out=runs[:, :, 0:WINDOW], in_=window2)
-        nc.vector.tensor_copy(out=runs[:, :, WINDOW : WINDOW + stay], in_=window3[:, :, 0:stay])
-        for above, row, rows in ((0, 1, WINDOW - 1), (WINDOW - 1, 0, 1)):
-            nc.vector.tensor_copy(
-                out=runs[:, above : above + rows, WINDOW + stay :],
-                in_=window3[:, row : row + rows, stay:],
-            )
+        nc.vector.tensor_copy(out=staying[:, :, 0:WINDOW], in_=window2)
+        nc.vector.tensor_copy(out=staying[:, :, WINDOW:stay], in_=window3[:, :, 0 : WINDOW - SHIFT])
+        nc.vector.tensor_copy(out=wrapping, in_=window3[:, :, WINDOW - SHIFT : WINDOW])
+        identity_bf16 = const.tile([P, P], BF16)
+        nc.vector.tensor_copy(out=identity_bf16[:], in_=identity[:])
 
         w_raw = keep.tile([P, TOKEN_TILES, K], BF16)
         a_raw = keep.tile([P, TOKEN_TILES, K], BF16)
@@ -124,44 +118,36 @@ def tile_swintransformerblock_pb_kernel(
             first = ((tau + 1) % TOKEN_TILES) * P
             return slice(first, first + P)
 
-        def load_x(group):
-            for tau in range(PAIR * group, PAIR * group + PAIR):
-                nc.sync.dma_start(out=x_sb[:, tau, :], in_=x_rows[output_rows(tau), :])
-
         load_block(a_raw, attn_rows, 0)
         load_block(a_raw, attn_rows, 1)
-        load_pair(w_raw, out_w, 0)
-        load_pair(w_raw, out_w, 1)
-        load_pair(a_raw, attn_rows, 1)
-        load_pair(w_raw, out_w, 2)
-        load_pair(w_raw, out_w, 3)
-        load_pair(a_raw, attn_rows, 2)
-        load_pair(a_raw, attn_rows, 3)
-        for group in range(GROUPS):
-            load_x(group)
+        load_block(w_raw, out_w, 0)
+        load_block(w_raw, out_w, 1)
+        for pair in range(1, GROUPS):
+            load_pair(w_raw, out_w, pair)
+        for group in range(1, GROUPS):
+            load_pair(a_raw, attn_rows, group)
+        for tau in range(TOKEN_TILES):
+            nc.sync.dma_start(out=x_sb[:, tau, :], in_=x_rows[output_rows(tau), :])
 
-        w_codes = keep.tile([P, PASSES, CHANNELS], U32, align_bytes=64)
-        w_scales = keep.tile([P, PASSES, CHANNELS], U8, align_bytes=64)
-        a_codes = keep.tile([P, PASSES, TOKENS], U32, align_bytes=64)
-        a_scales = keep.tile([P, PASSES, TOKENS], U8, align_bytes=64)
-        grouped = {}
+        w_codes = []
+        w_scales = []
+        for n in range(N_TILES):
+            w_codes.append(
+                keep.tile([P, PASSES, N_TILE], U32, name="w_codes%d" % n, align_bytes=64)
+            )
+            w_scales.append(
+                keep.tile([P, PASSES, N_TILE], U8, name="w_scales%d" % n, align_bytes=64)
+            )
+        w_grouped = {}
+        a_grouped = {}
+        turned = {}
+        a_codes = {}
+        a_scales = {}
 
-        def turned_pair(operand, pair):
+        def turn_weights(pair):
             banks = []
             for g in range(PASSES):
                 banks.append(psum_turned.tile([P, 2, PAIR * P], F32, name="turned"))
-                grouped[operand, pair, g] = work.tile(
-                    [P, PAIR * P, 4], BF16, name="grouped", align_bytes=64
-                )
-            return banks
-
-        def words_of(operand, pair, g):
-            return grouped[operand, pair, g][:].rearrange("p c t -> p (c t)").bitcast(F32).rearrange(
-                "p (c u) -> p c u", u=2
-            )
-
-        def turn_weights(pair, copies):
-            banks = turned_pair("w", pair)
             for half in range(PAIR):
                 columns = slice(half * P, (half + 1) * P)
                 transpose_block(
@@ -170,57 +156,107 @@ def tile_swintransformerblock_pb_kernel(
                     identity[:],
                     [[bank[:, u, columns] for u in range(2)] for bank in banks],
                 )
+            turned["w", pair] = banks
+
+        def group_weights(pair):
+            banks = turned["w", pair]
             for g in range(PASSES):
-                copies[g](
-                    out=words_of("w", pair, g), in_=banks[g][:].rearrange("p u c -> p c u")
+                w_grouped[pair, g] = work.tile(
+                    [P, PAIR * P, 4], BF16, name="w_grouped", align_bytes=64
+                )
+                nc.scalar.copy(
+                    out=w_grouped[pair, g][:].bitcast(F32),
+                    in_=banks[g][:].rearrange("p u c -> p c u"),
                 )
 
-        def turn_tokens(group, copies):
-            banks = turned_pair("a", group)
-            rows = [bank[:].rearrange("p u (r j) -> p u r j", j=GRID) for bank in banks]
+        def quantise_weights(pair):
+            columns = slice(PAIR * P * (pair % 2), PAIR * P * (pair % 2 + 1))
+            for g in range(PASSES):
+                nc.vector.quantize_mx(
+                    out=w_codes[pair // 2][:, g, columns].bitcast(FP8X4),
+                    scales=w_scales[pair // 2][:, g, columns],
+                    in_=w_grouped[pair, g][:].rearrange("p c t -> p (c t)"),
+                )
+
+        def turn_tokens(group):
+            halves = []
             for half, order in ((0, order_left), (1, order_right)):
-                columns = slice(half * 2 * WINDOW, (half + 1) * 2 * WINDOW)
+                bank = psum_turned.tile([P, PASSES, 2, P], F32, name="turned")
                 transpose_block(
                     nc,
                     a_raw[:, PAIR * group + half, :].bitcast(F32),
                     order[:],
-                    [[row[:, u, :, columns] for u in range(2)] for row in rows],
+                    [[bank[:, g, u, :] for u in range(2)] for g in range(PASSES)],
                 )
-            for g in range(PASSES):
-                words = words_of("a", group, g)
-                turned = banks[g][:].rearrange("p u c -> p c u")
-                copies[g](out=words[:, SHIFT:, :], in_=turned[:, : PAIR * P - SHIFT, :])
-                copies[g](out=words[:, :SHIFT, :], in_=turned[:, PAIR * P - SHIFT :, :])
+                halves.append(bank)
+            turned["a", group] = halves
 
-        def quantise(operand, pair, g):
-            codes, scales = (w_codes, w_scales) if operand == "w" else (a_codes, a_scales)
-            columns = slice(PAIR * P * pair, PAIR * P * (pair + 1))
-            nc.vector.quantize_mx(
-                out=codes[:, g, columns].bitcast(FP8X4),
-                scales=scales[:, g, columns],
-                in_=grouped[operand, pair, g][:].rearrange("p c t -> p (c t)"),
+        def group_tokens(group):
+            a_grouped[group] = work.tile(
+                [P, PASSES, PAIR * P, 4], BF16, name="a_grouped", align_bytes=64, bufs=GROUPS
+            )
+            grid = a_grouped[group][:].bitcast(F32).rearrange("p g (r j) u -> p g r j u", j=GRID)
+            left, right = turned["a", group]
+            nc.scalar.copy(
+                out=grid[:, :, :, SHIFT : SHIFT + 2 * WINDOW, :],
+                in_=left[:].rearrange("p g u (r j) -> p g r j u", j=2 * WINDOW),
+            )
+            nc.scalar.copy(
+                out=grid[:, :, :, GRID - stay : GRID, :],
+                in_=right[:, :, :, 0 : WINDOW * stay].rearrange("p g u (r j) -> p g r j u", j=stay),
+            )
+            nc.scalar.copy(
+                out=grid[:, :, :, 0:SHIFT, :],
+                in_=right[:, :, :, WINDOW * stay : P].rearrange("p g u (r j) -> p g r j u", j=SHIFT),
             )
 
-        bias_all = const.tile([P, CHANNELS], F32)
+        def quantise_tokens(group):
+            a_codes[group] = work.tile(
+                [P, PASSES, PAIR * P], U32, name="a_codes", align_bytes=64, bufs=GROUPS
+            )
+            a_scales[group] = work.tile(
+                [P, PASSES, PAIR * P], U8, name="a_scales", align_bytes=64, bufs=GROUPS
+            )
+            nc.vector.quantize_mx(
+                out=a_codes[group][:].rearrange("p g c -> p (g c)").bitcast(FP8X4),
+                scales=a_scales[group][:].rearrange("p g c -> p (g c)"),
+                in_=a_grouped[group][:].rearrange("p g c t -> p (g c t)"),
+            )
+
+        bias_all = const.tile([P, CHANNELS], BF16)
+        bias_columns = const.tile([P, TOKEN_TILES], BF16)
         ada = const.tile([P, 2, TOKEN_TILES + 1], F32)
         ada_gain = ada[:, 0, 1:]
         ada_offset = ada[:, 1, 1:]
         inv_ada_gain = const.tile([P, TOKEN_TILES], F32)
 
-        def spread_small_vectors():
-            for n in range(N_TILES):
-                columns = slice(n * N_TILE, (n + 1) * N_TILE)
-                spread = psum_acc.tile([P, N_TILE], F32, name="acc")
-                nc.tensor.matmul(
-                    out=spread[:], lhsT=ones[:], rhs=bias_row[:, columns], start=True, stop=True
-                )
-                nc.vector.tensor_copy(out=bias_all[:, columns], in_=spread[:])
-            ada_turned = psum_turned.tile([P, P], BF16, name="turned")
-            nc.tensor.transpose(ada_turned[:], ada_rows[:], identity_bf16[:])
-            vectors = ada_turned[:, 0 : 2 * TOKEN_TILES].rearrange("p (s t) -> p s t", s=2)
+        def turn_vectors():
+            columns = psum_acc.tile([P, P], BF16, name="acc")
+            nc.tensor.transpose(columns[:], vector_rows[:], identity_bf16[:])
+            turned["vectors"] = columns
+
+        def keep_vectors():
+            columns = turned["vectors"]
+            nc.vector.tensor_copy(
+                out=bias_columns[:], in_=columns[:, 2 * TOKEN_TILES : 3 * TOKEN_TILES]
+            )
+            vectors = columns[:, 0 : 2 * TOKEN_TILES].rearrange("p (s t) -> p s t", s=2)
             nc.vector.tensor_copy(out=ada[:, :, 0:TOKEN_TILES], in_=vectors)
             nc.vector.tensor_copy(out=ada[:, :, TOKEN_TILES:], in_=vectors[:, :, 0:1])
             nc.vector.reciprocal(out=inv_ada_gain[:], in_=ada_gain)
+
+        def spread_bias():
+            spread = psum_acc.tile([P, CHANNELS], BF16, name="acc")
+            for block in range(CHANNELS // P):
+                nc.tensor.transpose(
+                    spread[:, block * P : (block + 1) * P],
+                    bias_columns[:, block : block + 1].to_broadcast([P, P]),
+                    identity_bf16[:],
+                )
+            turned["bias"] = spread
+
+        def keep_bias():
+            nc.vector.tensor_copy(out=bias_all[:], in_=turned["bias"][:])
 
         sums = const.tile([P, TOKEN_TILES, N_TILES], F32)
         scaled_sums = const.tile([P, TOKEN_TILES, N_TILES], F32)
@@ -235,16 +271,15 @@ def tile_swintransformerblock_pb_kernel(
         acc = {}
 
         def matmuls(tau, n):
-            columns = slice(n * N_TILE, (n + 1) * N_TILE)
-            tokens = slice(tau * P, (tau + 1) * P)
+            group, tokens = tau // PAIR, slice((tau % PAIR) * P, (tau % PAIR + 1) * P)
             acc[tau, n] = psum_acc.tile([P, N_TILE], F32, name="acc")
             for g in range(PASSES):
                 nc.tensor.matmul_mx(
                     out=acc[tau, n][:],
-                    lhsT=a_codes[:, g, tokens].bitcast(FP8X4),
-                    lhsT_scale=a_scales[:, g, tokens],
-                    rhs=w_codes[:, g, columns].bitcast(FP8X4),
-                    rhs_scale=w_scales[:, g, columns],
+                    lhsT=a_codes[group][:, g, tokens].bitcast(FP8X4),
+                    lhsT_scale=a_scales[group][:, g, tokens],
+                    rhs=w_codes[n][:, g, :].bitcast(FP8X4),
+                    rhs_scale=w_scales[n][:, g, :],
                     start=(g == 0),
                     stop=(g == PASSES - 1),
                 )
@@ -252,7 +287,7 @@ def tile_swintransformerblock_pb_kernel(
         def add_bias(tau, n):
             columns = slice(n * N_TILE, (n + 1) * N_TILE)
             if n == 0:
-                projected[tau] = work.tile([P, CHANNELS], F32, name="projected", bufs=TOKEN_TILES)
+                projected[tau] = work.tile([P, CHANNELS], F32, name="projected")
             nc.vector.scalar_tensor_tensor(
                 out=projected[tau][:, columns],
                 in0=acc[tau, n][:],
@@ -263,7 +298,7 @@ def tile_swintransformerblock_pb_kernel(
                 accum_out=sums[:, tau, n : n + 1],
             )
 
-        def deviations(tau):
+        def mean(tau):
             nc.scalar.activation(
                 out=scaled_sums[:, tau, :],
                 in_=sums[:, tau, :],
@@ -271,6 +306,8 @@ def tile_swintransformerblock_pb_kernel(
                 scale=-1.0 / CHANNELS,
                 accum_out=minus_mean[:, tau : tau + 1],
             )
+
+        def square(tau):
             deviation_squared = work.tile([P, CHANNELS], BF16, name="deviation_squared", bufs=2)
             nc.scalar.activation(
                 out=deviation_squared[:],
@@ -316,7 +353,7 @@ def tile_swintransformerblock_pb_kernel(
                 )
 
         def shift_residual(tau):
-            result[tau] = work.tile([P, CHANNELS], F32, name="result", bufs=TOKEN_TILES)
+            result[tau] = work.tile([P, CHANNELS], F32, name="result")
             if tau < TOKEN_TILES // 2:
                 nc.gpsimd.tensor_scalar(
                     out=result[tau][:],
@@ -351,92 +388,105 @@ def tile_swintransformerblock_pb_kernel(
                     out=out_rows[output_rows(tau), columns], in_=result[tau][:, columns]
                 )
 
-        on_scalar = nc.scalar.copy
-        on_vector = nc.vector.tensor_copy
-
-        def quantise_pair(operand, pair):
-            for g in range(PASSES):
-                quantise(operand, pair, g)
-
         keep_clock_up(4)
-        turn_tokens(0, (on_scalar, on_vector))
-        quantise_pair("a", 0)
-        keep_clock_up(1)
-        turn_weights(0, (on_scalar, on_vector))
-        spread_small_vectors()
-        quantise_pair("w", 0)
-        turn_weights(1, (on_scalar, on_vector))
-        quantise_pair("w", 1)
-        keep_clock_up(1)
-        turn_tokens(1, (on_scalar, on_scalar))
-        keep_clock_up(1)
+        turn_tokens(0)
+        group_tokens(0)
+        quantise_tokens(0)
+        turn_weights(0)
+        group_weights(0)
+        turn_vectors()
+        keep_vectors()
+        quantise_weights(0)
+        turn_weights(1)
+        group_weights(1)
+        turn_weights(2)
+        quantise_weights(1)
+        group_weights(2)
+        spread_bias()
+        keep_bias()
+        turn_weights(3)
+        quantise_weights(2)
+        group_weights(3)
+        quantise_weights(3)
+        turn_tokens(1)
+        group_tokens(1)
         matmuls(0, 0)
         matmuls(1, 0)
         add_bias(0, 0)
+        quantise_tokens(1)
         add_bias(1, 0)
-        quantise_pair("a", 1)
-        turn_weights(2, (on_scalar, on_scalar))
-        matmuls(2, 0)
-        matmuls(3, 0)
-        quantise_pair("w", 2)
-        add_bias(2, 0)
-        add_bias(3, 0)
-        turn_weights(3, (on_scalar, on_scalar))
-        quantise_pair("w", 3)
-        turn_tokens(2, (on_scalar, on_scalar))
-        for tau in range(4):
-            matmuls(tau, 1)
+        turn_tokens(2)
+        group_tokens(2)
+        matmuls(0, 1)
+        matmuls(1, 1)
         add_bias(0, 1)
-        deviations(0)
         add_bias(1, 1)
-        deviations(1)
-        quantise_pair("a", 2)
-        deviation(0)
-        turn_tokens(3, (on_scalar, on_scalar))
+        mean(0)
+        mean(1)
+        square(0)
+        matmuls(2, 0)
+        matmuls(2, 1)
+        turn_tokens(3)
+        group_tokens(3)
+        matmuls(3, 0)
+        matmuls(3, 1)
+        add_bias(2, 0)
         add_bias(2, 1)
+        quantise_tokens(2)
+        mean(2)
+        square(1)
+        deviation(0)
+        add_bias(3, 0)
         add_bias(3, 1)
-        quantise_pair("a", 3)
-        deviations(2)
-        deviations(3)
-        deviation(1)
-        for tau in (4, 5):
-            for n in range(N_TILES):
-                matmuls(tau, n)
-        inverse_gain(0)
+        mean(3)
+        quantise_tokens(3)
+        square(2)
+        matmuls(4, 0)
+        matmuls(4, 1)
+        matmuls(5, 0)
+        matmuls(5, 1)
         add_bias(4, 0)
-        turn_gain(0)
+        inverse_gain(0)
         add_bias(4, 1)
+        turn_gain(0)
+        mean(4)
+        square(3)
+        deviation(1)
+        add_bias(5, 0)
         offsets(0)
         shift_residual(0)
         shift_residual(1)
-        deviations(4)
-        add_bias(5, 0)
-        inverse_gain(1)
         add_bias(5, 1)
-        turn_gain(1)
-        deviations(5)
-        deviation(2)
-        for tau in (6, 7):
-            for n in range(N_TILES):
-                matmuls(tau, n)
+        mean(5)
+        square(4)
+        matmuls(6, 0)
+        matmuls(6, 1)
+        matmuls(7, 0)
+        matmuls(7, 1)
         add_bias(6, 0)
+        inverse_gain(1)
+        add_bias(6, 1)
+        turn_gain(1)
+        mean(6)
+        square(5)
+        deviation(2)
         offsets(1)
+        finish(0)
         shift_residual(2)
         shift_residual(3)
-        add_bias(6, 1)
-        deviations(6)
         add_bias(7, 0)
         add_bias(7, 1)
-        deviations(7)
+        mean(7)
+        square(6)
+        square(7)
         deviation(3)
-        finish(0)
         inverse_gain(2)
         finish(1)
         turn_gain(2)
-        finish(2)
         offsets(2)
         shift_residual(4)
         shift_residual(5)
+        finish(2)
         inverse_gain(3)
         finish(3)
         turn_gain(3)

@@ -390,20 +390,24 @@ def tile_swintransformerblock_pb_kernel(
 
         keep_clock_up(4)
         turn_tokens(0)
+        keep_clock_up(1)
         group_tokens(0)
         quantise_tokens(0)
         turn_weights(0)
         group_weights(0)
         turn_vectors()
+        keep_clock_up(1)
         keep_vectors()
         quantise_weights(0)
         turn_weights(1)
         group_weights(1)
+        keep_clock_up(1)
         turn_weights(2)
         quantise_weights(1)
         group_weights(2)
         spread_bias()
         keep_bias()
+        keep_clock_up(1)
         turn_weights(3)
         quantise_weights(2)
         group_weights(3)

@@ -53,6 +53,19 @@ def tile_swintransformerblock_pb_kernel(
         psum_acc = stack.enter_context(tc.psum_pool(name="psum_acc", bufs=4))
         stack.enter_context(tc.manual_schedule())
 
+        vector_rows = const.tile([P, P], BF16)
+        nc.vector.memset(vector_rows[:].bitcast(U32), 0)
+        for index, rows in enumerate(
+            (
+                ada1_scale.rearrange("o (t p) i -> (o t) (p i)", p=P),
+                ada1_shift.rearrange("o (t p) i -> (o t) (p i)", p=P),
+            )
+        ):
+            nc.scalar.dma_start(out=vector_rows[8 * index : 8 * (index + 1), :], in_=rows)
+        bias_row = const.tile([P, CHANNELS], BF16)
+        nc.vector.memset(bias_row[:].bitcast(U32), 0)
+        nc.scalar.dma_start(out=bias_row[0:1, :], in_=out_b.unsqueeze(0))
+
         warm = const.tile([P, 1], F32)
         nc.vector.memset(warm[:], 1.0)
         nc.scalar.activation(out=warm[:], in_=warm[:], func=ACT.Sqrt)
@@ -66,17 +79,6 @@ def tile_swintransformerblock_pb_kernel(
                 nc.tensor.matmul(
                     out=idle[:], lhsT=filler[:, 0:P], rhs=filler[:], start=True, stop=True
                 )
-
-        vector_rows = const.tile([P, P], BF16)
-        nc.vector.memset(vector_rows[:].bitcast(U32), 0)
-        for index, rows in enumerate(
-            (
-                ada1_scale.rearrange("o (t p) i -> (o t) (p i)", p=P),
-                ada1_shift.rearrange("o (t p) i -> (o t) (p i)", p=P),
-                out_b.rearrange("(t p) -> t p", p=P),
-            )
-        ):
-            nc.scalar.dma_start(out=vector_rows[8 * index : 8 * (index + 1), :], in_=rows)
 
         identity = const.tile([P, P], F32)
         make_identity(nc, identity[:])
@@ -95,6 +97,8 @@ def tile_swintransformerblock_pb_kernel(
         nc.vector.tensor_copy(out=staying[:, :, 0:WINDOW], in_=window2)
         nc.vector.tensor_copy(out=staying[:, :, WINDOW:stay], in_=window3[:, :, 0 : WINDOW - SHIFT])
         nc.vector.tensor_copy(out=wrapping, in_=window3[:, :, WINDOW - SHIFT : WINDOW])
+        ones = const.tile([P, P], BF16)
+        nc.vector.memset(ones[:], 1.0)
         identity_bf16 = const.tile([P, P], BF16)
         nc.vector.tensor_copy(out=identity_bf16[:], in_=identity[:])
 
@@ -158,13 +162,13 @@ def tile_swintransformerblock_pb_kernel(
                 )
             turned["w", pair] = banks
 
-        def group_weights(pair):
+        def group_weights(pair, copies):
             banks = turned["w", pair]
             for g in range(PASSES):
                 w_grouped[pair, g] = work.tile(
                     [P, PAIR * P, 4], BF16, name="w_grouped", align_bytes=64
                 )
-                nc.scalar.copy(
+                copies[g](
                     out=w_grouped[pair, g][:].bitcast(F32),
                     in_=banks[g][:].rearrange("p u c -> p c u"),
                 )
@@ -191,21 +195,21 @@ def tile_swintransformerblock_pb_kernel(
                 halves.append(bank)
             turned["a", group] = halves
 
-        def group_tokens(group):
+        def group_tokens(group, copies):
             a_grouped[group] = work.tile(
                 [P, PASSES, PAIR * P, 4], BF16, name="a_grouped", align_bytes=64, bufs=GROUPS
             )
             grid = a_grouped[group][:].bitcast(F32).rearrange("p g (r j) u -> p g r j u", j=GRID)
             left, right = turned["a", group]
-            nc.scalar.copy(
+            copies[0](
                 out=grid[:, :, :, SHIFT : SHIFT + 2 * WINDOW, :],
                 in_=left[:].rearrange("p g u (r j) -> p g r j u", j=2 * WINDOW),
             )
-            nc.scalar.copy(
+            copies[1](
                 out=grid[:, :, :, GRID - stay : GRID, :],
                 in_=right[:, :, :, 0 : WINDOW * stay].rearrange("p g u (r j) -> p g r j u", j=stay),
             )
-            nc.scalar.copy(
+            copies[1](
                 out=grid[:, :, :, 0:SHIFT, :],
                 in_=right[:, :, :, WINDOW * stay : P].rearrange("p g u (r j) -> p g r j u", j=SHIFT),
             )
@@ -224,7 +228,6 @@ def tile_swintransformerblock_pb_kernel(
             )
 
         bias_all = const.tile([P, CHANNELS], BF16)
-        bias_columns = const.tile([P, TOKEN_TILES], BF16)
         ada = const.tile([P, 2, TOKEN_TILES + 1], F32)
         ada_gain = ada[:, 0, 1:]
         ada_offset = ada[:, 1, 1:]
@@ -237,26 +240,25 @@ def tile_swintransformerblock_pb_kernel(
 
         def keep_vectors():
             columns = turned["vectors"]
-            nc.vector.tensor_copy(
-                out=bias_columns[:], in_=columns[:, 2 * TOKEN_TILES : 3 * TOKEN_TILES]
-            )
             vectors = columns[:, 0 : 2 * TOKEN_TILES].rearrange("p (s t) -> p s t", s=2)
             nc.vector.tensor_copy(out=ada[:, :, 0:TOKEN_TILES], in_=vectors)
             nc.vector.tensor_copy(out=ada[:, :, TOKEN_TILES:], in_=vectors[:, :, 0:1])
             nc.vector.reciprocal(out=inv_ada_gain[:], in_=ada_gain)
 
-        def spread_bias():
-            spread = psum_acc.tile([P, CHANNELS], BF16, name="acc")
-            for block in range(CHANNELS // P):
-                nc.tensor.transpose(
-                    spread[:, block * P : (block + 1) * P],
-                    bias_columns[:, block : block + 1].to_broadcast([P, P]),
-                    identity_bf16[:],
-                )
-            turned["bias"] = spread
+        def spread_bias(n):
+            columns = slice(n * N_TILE, (n + 1) * N_TILE)
+            turned["bias", n] = psum_acc.tile([P, N_TILE], F32, name="acc")
+            nc.tensor.matmul(
+                out=turned["bias", n][:],
+                lhsT=ones[:],
+                rhs=bias_row[:, columns],
+                start=True,
+                stop=True,
+            )
 
-        def keep_bias():
-            nc.vector.tensor_copy(out=bias_all[:], in_=turned["bias"][:])
+        def keep_bias(n):
+            columns = slice(n * N_TILE, (n + 1) * N_TILE)
+            nc.vector.tensor_copy(out=bias_all[:, columns], in_=turned["bias", n][:])
 
         sums = const.tile([P, TOKEN_TILES, N_TILES], F32)
         scaled_sums = const.tile([P, TOKEN_TILES, N_TILES], F32)
@@ -354,7 +356,7 @@ def tile_swintransformerblock_pb_kernel(
 
         def shift_residual(tau):
             result[tau] = work.tile([P, CHANNELS], F32, name="result")
-            if tau < TOKEN_TILES // 2:
+            if tau in (0, 1, 2):
                 nc.gpsimd.tensor_scalar(
                     out=result[tau][:],
                     in0=x_sb[:, tau, :],
@@ -388,39 +390,41 @@ def tile_swintransformerblock_pb_kernel(
                     out=out_rows[output_rows(tau), columns], in_=result[tau][:, columns]
                 )
 
-        keep_clock_up(4)
+        both = (nc.scalar.copy, nc.scalar.copy)
+        keep_clock_up(3)
         turn_tokens(0)
         keep_clock_up(1)
-        group_tokens(0)
+        group_tokens(0, both)
         quantise_tokens(0)
         turn_weights(0)
-        group_weights(0)
+        group_weights(0, both)
         turn_vectors()
-        keep_clock_up(1)
+        spread_bias(0)
         keep_vectors()
+        keep_bias(0)
         quantise_weights(0)
         turn_weights(1)
-        group_weights(1)
-        keep_clock_up(1)
+        group_weights(1, both)
+        spread_bias(1)
         turn_weights(2)
         quantise_weights(1)
-        group_weights(2)
-        spread_bias()
-        keep_bias()
+        keep_bias(1)
+        group_weights(2, both)
         keep_clock_up(1)
         turn_weights(3)
         quantise_weights(2)
-        group_weights(3)
+        group_weights(3, both)
+        keep_clock_up(1)
         quantise_weights(3)
         turn_tokens(1)
-        group_tokens(1)
+        group_tokens(1, both)
         matmuls(0, 0)
         matmuls(1, 0)
         add_bias(0, 0)
         quantise_tokens(1)
         add_bias(1, 0)
         turn_tokens(2)
-        group_tokens(2)
+        group_tokens(2, both)
         matmuls(0, 1)
         matmuls(1, 1)
         add_bias(0, 1)
@@ -431,7 +435,7 @@ def tile_swintransformerblock_pb_kernel(
         matmuls(2, 0)
         matmuls(2, 1)
         turn_tokens(3)
-        group_tokens(3)
+        group_tokens(3, both)
         matmuls(3, 0)
         matmuls(3, 1)
         add_bias(2, 0)
@@ -484,15 +488,15 @@ def tile_swintransformerblock_pb_kernel(
         square(6)
         square(7)
         deviation(3)
-        inverse_gain(2)
         finish(1)
+        inverse_gain(2)
+        finish(2)
         turn_gain(2)
         offsets(2)
         shift_residual(4)
         shift_residual(5)
-        finish(2)
-        inverse_gain(3)
         finish(3)
+        inverse_gain(3)
         turn_gain(3)
         offsets(3)
         shift_residual(6)

from contextlib import ExitStack

import concourse.mybir as mybir
from concourse.masks import make_identity

F32 = mybir.dt.float32
BF16 = mybir.dt.bfloat16
U32 = mybir.dt.uint32
U8 = mybir.dt.uint8
FP8X4 = mybir.dt.float8_e4m3fn_x4
ALU = mybir.AluOpType
ACT = mybir.ActivationFunctionType

P = 128
TOKENS = 1024
CHANNELS = 1024
K = 1024
K_PASS = 4 * P
PASSES = K // K_PASS
N_TILE = 512
N_TILES = CHANNELS // N_TILE
TOKEN_TILES = TOKENS // P
GRID = 32
WINDOW = 8
SHIFT = 4
PAIR = 2
GROUPS = TOKEN_TILES // PAIR
EPS = 1e-5

FLOPS = 2 * TOKENS * CHANNELS * K


def transpose_block(nc, words, order, places):
    for g in range(PASSES):
        for u in range(2):
            every_second = slice(2 * P * g + u, 2 * P * (g + 1), 2)
            nc.tensor.transpose(places[g][u], words[:, every_second], order)


def tile_swintransformerblock_pb_kernel(
    tc, o_attn, out_w, out_b, ada1_scale, ada1_shift, x, out
):
    nc = tc.nc
    attn_rows = o_attn.flatten_outer_dims()
    x_rows = x.flatten_outer_dims()
    out_rows = out.flatten_outer_dims()

    with ExitStack() as stack:
        const = stack.enter_context(tc.tile_pool(name="const", bufs=1))
        keep = stack.enter_context(tc.tile_pool(name="keep", bufs=1))
        work = stack.enter_context(tc.tile_pool(name="work", bufs=TOKEN_TILES))
        psum_turned = stack.enter_context(tc.psum_pool(name="psum_turned", bufs=4))
        psum_acc = stack.enter_context(tc.psum_pool(name="psum_acc", bufs=4))
        stack.enter_context(tc.manual_schedule())

        vector_rows = const.tile([P, P], BF16)
        nc.vector.memset(vector_rows[:].bitcast(U32), 0)
        for index, rows in enumerate(
            (
                ada1_scale.rearrange("o (t p) i -> (o t) (p i)", p=P),
                ada1_shift.rearrange("o (t p) i -> (o t) (p i)", p=P),
            )
        ):
            nc.scalar.dma_start(out=vector_rows[8 * index : 8 * (index + 1), :], in_=rows)
        bias_row = const.tile([P, CHANNELS], BF16)
        nc.vector.memset(bias_row[:].bitcast(U32), 0)
        nc.scalar.dma_start(out=bias_row[0:1, :], in_=out_b.unsqueeze(0))

        warm = const.tile([P, 1], F32)
        nc.vector.memset(warm[:], 1.0)
        nc.scalar.activation(out=warm[:], in_=warm[:], func=ACT.Sqrt)

        filler = const.tile([P, N_TILE], BF16)
        nc.vector.memset(filler[:].bitcast(U32), 0)

        def keep_clock_up(times):
            for step in range(times):
                idle = psum_acc.tile([P, N_TILE], F32, name="acc")
                nc.tensor.matmul(
                    out=idle[:], lhsT=filler[:, 0:P], rhs=filler[:], start=True, stop=True
                )

        identity = const.tile([P, P], F32)
        make_identity(nc, identity[:])

        order_left = const.tile([P, P], F32)
        nc.vector.tensor_copy(
            out=order_left[:].rearrange("p (r d c) -> p r d c", r=WINDOW, d=2),
            in_=identity[:].rearrange("p (d r c) -> p r d c", d=2, r=WINDOW),
        )
        stay = 2 * WINDOW - SHIFT
        order_right = const.tile([P, P], F32)
        staying = order_right[:, 0 : WINDOW * stay].rearrange("p (r j) -> p r j", j=stay)
        wrapping = order_right[:, WINDOW * stay : P].rearrange("p (r j) -> p r j", j=SHIFT)
        window2 = identity[:, 0:64].rearrange("p (r c) -> p r c", c=WINDOW)
        window3 = identity[:, 64:128].rearrange("p (r c) -> p r c", c=WINDOW)
        nc.vector.tensor_copy(out=staying[:, :, 0:WINDOW], in_=window2)
        nc.vector.tensor_copy(out=staying[:, :, WINDOW:stay], in_=window3[:, :, 0 : WINDOW - SHIFT])
        nc.vector.tensor_copy(out=wrapping, in_=window3[:, :, WINDOW - SHIFT : WINDOW])
        ones = const.tile([P, P], BF16)
        nc.vector.memset(ones[:], 1.0)
        identity_bf16 = const.tile([P, P], BF16)
        nc.vector.tensor_copy(out=identity_bf16[:], in_=identity[:])

        w_raw = keep.tile([P, TOKEN_TILES, K], BF16)
        a_raw = keep.tile([P, TOKEN_TILES, K], BF16)
        x_sb = keep.tile([P, TOKEN_TILES, CHANNELS], BF16)

        def load_block(raw, rows, block):
            nc.sync.dma_start(out=raw[:, block, :], in_=rows[P * block : P * (block + 1), :])

        def load_pair(raw, rows, pair):
            blocks = slice(PAIR * pair, PAIR * pair + PAIR)
            nc.sync.dma_start(
                out=raw[:, blocks, :],
                in_=rows[PAIR * P * pair : PAIR * P * (pair + 1), :].rearrange(
                    "(b p) k -> p b k", p=P
                ),
            )

        def output_rows(tau):
            first = ((tau + 1) % TOKEN_TILES) * P
            return slice(first, first + P)

        load_block(a_raw, attn_rows, 0)
        load_block(a_raw, attn_rows, 1)
        load_block(w_raw, out_w, 0)
        load_block(w_raw, out_w, 1)
        for pair in range(1, GROUPS):
            load_pair(w_raw, out_w, pair)
        for group in range(1, GROUPS):
            load_pair(a_raw, attn_rows, group)
        for tau in range(TOKEN_TILES):
            nc.sync.dma_start(out=x_sb[:, tau, :], in_=x_rows[output_rows(tau), :])

        w_codes = []
        w_scales = []
        for n in range(N_TILES):
            w_codes.append(
                keep.tile([P, PASSES, N_TILE], U32, name="w_codes%d" % n, align_bytes=64)
            )
            w_scales.append(
                keep.tile([P, PASSES, N_TILE], U8, name="w_scales%d" % n, align_bytes=64)
            )
        w_grouped = {}
        a_grouped = {}
        turned = {}
        a_codes = {}
        a_scales = {}

        def turn_weights(pair):
            banks = []
            for g in range(PASSES):
                banks.append(psum_turned.tile([P, 2, PAIR * P], F32, name="turned"))
            for half in range(PAIR):
                columns = slice(half * P, (half + 1) * P)
                transpose_block(
                    nc,
                    w_raw[:, PAIR * pair + half, :].bitcast(F32),
                    identity[:],
                    [[bank[:, u, columns] for u in range(2)] for bank in banks],
                )
            turned["w", pair] = banks

        def group_weights(pair, copies):
            banks = turned["w", pair]
            for g in range(PASSES):
                w_grouped[pair, g] = work.tile(
                    [P, PAIR * P, 4], BF16, name="w_grouped", align_bytes=64
                )
                copies[g](
                    out=w_grouped[pair, g][:].bitcast(F32),
                    in_=banks[g][:].rearrange("p u c -> p c u"),
                )

        def quantise_weights(pair):
            columns = slice(PAIR * P * (pair % 2), PAIR * P * (pair % 2 + 1))
            for g in range(PASSES):
                nc.vector.quantize_mx(
                    out=w_codes[pair // 2][:, g, columns].bitcast(FP8X4),
                    scales=w_scales[pair // 2][:, g, columns],
                    in_=w_grouped[pair, g][:].rearrange("p c t -> p (c t)"),
                )

        def turn_tokens(group):
            halves = []
            for half, order in ((0, order_left), (1, order_right)):
                bank = psum_turned.tile([P, PASSES, 2, P], F32, name="turned")
                transpose_block(
                    nc,
                    a_raw[:, PAIR * group + half, :].bitcast(F32),
                    order[:],
                    [[bank[:, g, u, :] for u in range(2)] for g in range(PASSES)],
                )
                halves.append(bank)
            turned["a", group] = halves

        def group_tokens(group, copies):
            a_grouped[group] = work.tile(
                [P, PASSES, PAIR * P, 4], BF16, name="a_grouped", align_bytes=64, bufs=GROUPS
            )
            grid = a_grouped[group][:].bitcast(F32).rearrange("p g (r j) u -> p g r j u", j=GRID)
            left, right = turned["a", group]
            copies[0](
                out=grid[:, :, :, SHIFT : SHIFT + 2 * WINDOW, :],
                in_=left[:].rearrange("p g u (r j) -> p g r j u", j=2 * WINDOW),
            )
            copies[1](
                out=grid[:, :, :, GRID - stay : GRID, :],
                in_=right[:, :, :, 0 : WINDOW * stay].rearrange("p g u (r j) -> p g r j u", j=stay),
            )
            copies[1](
                out=grid[:, :, :, 0:SHIFT, :],
                in_=right[:, :, :, WINDOW * stay : P].rearrange("p g u (r j) -> p g r j u", j=SHIFT),
            )

        def quantise_tokens(group):
            a_codes[group] = work.tile(
                [P, PASSES, PAIR * P], U32, name="a_codes", align_bytes=64, bufs=GROUPS
            )
            a_scales[group] = work.tile(
                [P, PASSES, PAIR * P], U8, name="a_scales", align_bytes=64, bufs=GROUPS
            )
            nc.vector.quantize_mx(
                out=a_codes[group][:].rearrange("p g c -> p (g c)").bitcast(FP8X4),
                scales=a_scales[group][:].rearrange("p g c -> p (g c)"),
                in_=a_grouped[group][:].rearrange("p g c t -> p (g c t)"),
            )

        bias_all = const.tile([P, CHANNELS], BF16)
        ada = const.tile([P, 2, TOKEN_TILES + 1], F32)
        ada_gain = ada[:, 0, 1:]
        ada_offset = ada[:, 1, 1:]
        inv_ada_gain = const.tile([P, TOKEN_TILES], F32)

        def turn_vectors():
            columns = psum_acc.tile([P, P], BF16, name="acc")
            nc.tensor.transpose(columns[:], vector_rows[:], identity_bf16[:])
            turned["vectors"] = columns

        def keep_vectors():
            columns = turned["vectors"]
            vectors = columns[:, 0 : 2 * TOKEN_TILES].rearrange("p (s t) -> p s t", s=2)
            nc.vector.tensor_copy(out=ada[:, :, 0:TOKEN_TILES], in_=vectors)
            nc.vector.tensor_copy(out=ada[:, :, TOKEN_TILES:], in_=vectors[:, :, 0:1])
            nc.vector.reciprocal(out=inv_ada_gain[:], in_=ada_gain)

        def spread_bias(n):
            columns = slice(n * N_TILE, (n + 1) * N_TILE)
            turned["bias", n] = psum_acc.tile([P, N_TILE], F32, name="acc")
            nc.tensor.matmul(
                out=turned["bias", n][:],
                lhsT=ones[:],
                rhs=bias_row[:, columns],
                start=True,
                stop=True,
            )

        def keep_bias(n):
            columns = slice(n * N_TILE, (n + 1) * N_TILE)
            nc.vector.tensor_copy(out=bias_all[:, columns], in_=turned["bias", n][:])

        sums = const.tile([P, TOKEN_TILES, N_TILES], F32)
        scaled_sums = const.tile([P, TOKEN_TILES, N_TILES], F32)
        minus_mean = const.tile([P, TOKEN_TILES], F32)
        squares = const.tile([P, TOKEN_TILES], F32)
        std = const.tile([P, TOKEN_TILES], F32)
        gain = const.tile([P, TOKEN_TILES], F32)
        offset = const.tile([P, TOKEN_TILES], F32)
        projected = {}
        result = {}

        acc = {}

        def matmuls(tau, n):
            group, tokens = tau // PAIR, slice((tau % PAIR) * P, (tau % PAIR + 1) * P)
            acc[tau, n] = psum_acc.tile([P, N_TILE], F32, name="acc")
            for g in range(PASSES):
                nc.tensor.matmul_mx(
                    out=acc[tau, n][:],
                    lhsT=a_codes[group][:, g, tokens].bitcast(FP8X4),
                    lhsT_scale=a_scales[group][:, g, tokens],
                    rhs=w_codes[n][:, g, :].bitcast(FP8X4),
                    rhs_scale=w_scales[n][:, g, :],
                    start=(g == 0),
                    stop=(g == PASSES - 1),
                )

        def add_bias(tau, n):
            columns = slice(n * N_TILE, (n + 1) * N_TILE)
            if n == 0:
                projected[tau] = work.tile([P, CHANNELS], F32, name="projected")
            nc.vector.scalar_tensor_tensor(
                out=projected[tau][:, columns],
                in0=acc[tau, n][:],
                scalar=1.0,
                in1=bias_all[:, columns],
                op0=ALU.mult,
                op1=ALU.add,
                accum_out=sums[:, tau, n : n + 1],
            )

        def mean(tau):
            nc.scalar.activation(
                out=scaled_sums[:, tau, :],
                in_=sums[:, tau, :],
                func=ACT.Identity,
                scale=-1.0 / CHANNELS,
                accum_out=minus_mean[:, tau : tau + 1],
            )

        def square(tau):
            deviation_squared = work.tile([P, CHANNELS], BF16, name="deviation_squared", bufs=2)
            nc.scalar.activation(
                out=deviation_squared[:],
                in_=projected[tau][:],
                func=ACT.Square,
                bias=minus_mean[:, tau : tau + 1],
                accum_out=squares[:, tau : tau + 1],
            )

        def pair_columns(group):
            return slice(PAIR * group, PAIR * group + PAIR)

        def deviation(group):
            pair = pair_columns(group)
            nc.scalar.activation(
                out=std[:, pair], in_=squares[:, pair], func=ACT.Sqrt, scale=1.0 / (CHANNELS - 1)
            )

        def inverse_gain(group):
            pair = pair_columns(group)
            nc.vector.scalar_tensor_tensor(
                out=gain[:, pair],
                in0=std[:, pair],
                scalar=EPS,
                in1=inv_ada_gain[:, pair],
                op0=ALU.add,
                op1=ALU.mult,
            )

        def turn_gain(group):
            pair = pair_columns(group)
            nc.vector.reciprocal(out=gain[:, pair], in_=gain[:, pair])

        def offsets(group):
            for tau in range(PAIR * group, PAIR * group + PAIR):
                nc.vector.tensor_scalar(
                    out=offset[:, tau : tau + 1],
                    in0=minus_mean[:, tau : tau + 1],
                    scalar1=gain[:, tau : tau + 1],
                    scalar2=ada_offset[:, tau : tau + 1],
                    op0=ALU.mult,
                    op1=ALU.add,
                )

        def shift_residual(tau):
            result[tau] = work.tile([P, CHANNELS], F32, name="result")
            if tau in (0, 1, 2):
                nc.gpsimd.tensor_scalar(
                    out=result[tau][:],
                    in0=x_sb[:, tau, :],
                    scalar1=1.0,
                    scalar2=offset[:, tau : tau + 1],
                    op0=ALU.mult,
                    op1=ALU.add,
                )
            else:
                nc.scalar.activation(
                    out=result[tau][:],
                    in_=x_sb[:, tau, :],
                    func=ACT.Identity,
                    bias=offset[:, tau : tau + 1],
                )

        def finish(tau):
            pieces = 2 if tau == TOKEN_TILES - 1 else 1
            width = CHANNELS // pieces
            for piece in range(pieces):
                columns = slice(piece * width, (piece + 1) * width)
                nc.vector.scalar_tensor_tensor(
                    out=result[tau][:, columns],
                    in0=projected[tau][:, columns],
                    scalar=gain[:, tau : tau + 1],
                    in1=result[tau][:, columns],
                    op0=ALU.mult,
                    op1=ALU.add,
                )
                nc.sync.dma_start(
                    out=out_rows[output_rows(tau), columns], in_=result[tau][:, columns]
                )

        both = (nc.scalar.copy, nc.scalar.copy)
        keep_clock_up(3)
        turn_tokens(0)
        keep_clock_up(1)
        group_tokens(0, both)
        quantise_tokens(0)
        turn_weights(0)
        group_weights(0, both)
        turn_vectors()
        spread_bias(0)
        keep_vectors()
        keep_bias(0)
        quantise_weights(0)
        turn_weights(1)
        group_weights(1, both)
        spread_bias(1)
        turn_weights(2)
        quantise_weights(1)
        keep_bias(1)
        group_weights(2, both)
        keep_clock_up(1)
        turn_weights(3)
        quantise_weights(2)
        group_weights(3, both)
        keep_clock_up(1)
        quantise_weights(3)
        turn_tokens(1)
        group_tokens(1, both)
        matmuls(0, 0)
        matmuls(1, 0)
        add_bias(0, 0)
        quantise_tokens(1)
        add_bias(1, 0)
        turn_tokens(2)
        group_tokens(2, both)
        matmuls(0, 1)
        matmuls(1, 1)
        add_bias(0, 1)
        add_bias(1, 1)
        mean(0)
        mean(1)
        square(0)
        matmuls(2, 0)
        matmuls(2, 1)
        turn_tokens(3)
        group_tokens(3, both)
        matmuls(3, 0)
        matmuls(3, 1)
        add_bias(2, 0)
        add_bias(2, 1)
        quantise_tokens(2)
        mean(2)
        square(1)
        deviation(0)
        add_bias(3, 0)
        add_bias(3, 1)
        mean(3)
        quantise_tokens(3)
        square(2)
        matmuls(4, 0)
        matmuls(4, 1)
        matmuls(5, 0)
        matmuls(5, 1)
        add_bias(4, 0)
        inverse_gain(0)
        add_bias(4, 1)
        turn_gain(0)
        mean(4)
        square(3)
        deviation(1)
        add_bias(5, 0)
        offsets(0)
        shift_residual(0)
        shift_residual(1)
        add_bias(5, 1)
        mean(5)
        square(4)
        matmuls(6, 0)
        matmuls(6, 1)
        matmuls(7, 0)
        matmuls(7, 1)
        add_bias(6, 0)
        inverse_gain(1)
        add_bias(6, 1)
        turn_gain(1)
        mean(6)
        square(5)
        deviation(2)
        offsets(1)
        finish(0)
        shift_residual(2)
        shift_residual(3)
        add_bias(7, 0)
        add_bias(7, 1)
        mean(7)
        square(6)
        square(7)
        deviation(3)
        finish(1)
        inverse_gain(2)
        finish(2)
        turn_gain(2)
        offsets(2)
        shift_residual(4)
        shift_residual(5)
        finish(3)
        inverse_gain(3)
        turn_gain(3)
        offsets(3)
        shift_residual(6)
        shift_residual(7)
        finish(4)
        finish(5)
        finish(6)
        finish(7)
